import numpy as np
import ml_dtypes


def mxq(x, axis, fmt="e4m3"):
    dtype, down = {"e4m3": (ml_dtypes.float8_e4m3fn, 7), "e5m2": (ml_dtypes.float8_e5m2, 14)}[fmt]
    v = np.moveaxis(np.asarray(x, np.float32).astype(ml_dtypes.bfloat16).astype(np.float64), axis, -1)
    blocks = v.reshape(v.shape[:-1] + (-1, 32))
    amax = np.abs(blocks).max(-1, keepdims=True)
    byte = np.maximum(np.where(amax > 0, np.frexp(amax)[1] - 1 + 127, 0) - down, 1)
    scale = np.exp2(byte - 127.0)
    codes = (blocks / scale).astype(np.float32).astype(dtype).astype(np.float64)
    return np.moveaxis((codes * scale).reshape(v.shape), -1, axis)


WIDE = False


def mx_kscale(k):
    if not WIDE:
        return np.ones(k)
    levels = np.array([10, -10, 5, -5, 0])
    a = np.random.permutation(np.resize(levels, k // 512 * 4)).reshape(k // 512, 4)
    idx = np.arange(k)
    return np.exp2(a[idx // 512, idx % 128 // 32])


BF16 = ml_dtypes.bfloat16


def bf(x):
    return np.asarray(x, np.float32).astype(BF16)


def f64(x):
    return np.asarray(x).astype(np.float64)


B, L_IMG, L_TXT, DM, H, D = 1, 6144, 2048, 512, 2, 64
L = L_TXT + L_IMG
HD = H * D
EPS = 1e-6


def rms(x, gain):
    return x / np.sqrt(np.mean(np.square(x), axis=-1, keepdims=True) + EPS) * gain


def qkv(x, w, qn, kn):
    y = (mxq(x, 2, "e4m3") @ mxq(w, 0, "e4m3")).reshape(x.shape[0], x.shape[1], 3, H, D)
    return rms(y[:, :, 0], qn), rms(y[:, :, 1], kn), y[:, :, 2]


def rope(x, fc):
    x_ = x.reshape(x.shape[:-1] + (D // 2, 1, 2))
    out = fc[:, None, :, :, 0] * x_[..., 0] + fc[:, None, :, :, 1] * x_[..., 1]
    return out.reshape(x.shape)


def setup_inputs():
    s = mx_kscale(DM)
    r = np.random.standard_normal
    return {
        "hidden_states": bf(r((B, L_IMG, DM)) * s),
        "encoder_hidden_states": bf(r((B, L_TXT, DM)) * s),
        "image_rotary_emb": bf(r((L, D // 2, 4)) * 0.6),
        "W_iqkv": bf(r((DM, 3 * HD)) / np.sqrt(DM) / s[:, None]),
        "W_eqkv": bf(r((DM, 3 * HD)) / np.sqrt(DM) / s[:, None]),
        "qn_scale": bf(1.0 + 0.1 * r(D)),
        "kn_scale": bf(1.0 + 0.1 * r(D)),
        "eqn_scale": bf(1.0 + 0.1 * r(D)),
        "ekn_scale": bf(1.0 + 0.1 * r(D)),
    }


def reference(hidden_states, encoder_hidden_states, image_rotary_emb, W_iqkv, W_eqkv, qn_scale, kn_scale, eqn_scale, ekn_scale):
    q, k, v = qkv(f64(hidden_states), f64(W_iqkv), f64(qn_scale), f64(kn_scale))
    eq, ek, ev = qkv(f64(encoder_hidden_states), f64(W_eqkv), f64(eqn_scale), f64(ekn_scale))
    q = np.concatenate((eq, q), axis=1)
    k = np.concatenate((ek, k), axis=1)
    v = np.concatenate((ev, v), axis=1)
    fc = f64(image_rotary_emb).reshape(L, D // 2, 2, 2)
    return rope(q, fc).reshape(B, L, HD), rope(k, fc).reshape(B, L, HD), v.reshape(B, L, HD)

@@ -1,0 +1,339 @@
+from contextlib import ExitStack
+
+import concourse.mybir as mybir
+from concourse.masks import make_identity
+
+FLOPS = 2 * 8192 * 512 * 384
+
+F32 = mybir.dt.float32
+BF16 = mybir.dt.bfloat16
+U32 = mybir.dt.uint32
+U8 = mybir.dt.uint8
+FP8X4 = mybir.dt.float8_e4m3fn_x4
+ALU = mybir.AluOpType
+ACT = mybir.ActivationFunctionType
+
+P = 128
+EPS = 1e-6
+GROUP_TILES = 8
+N_GROUPS = 8
+TEXT_GROUPS = 2
+UNIT_TILES = (2, 2, 4, 4, 4, 4, 4, 4, 4, 4, 4, 4, 4, 4, 4, 4, 2, 2)
+GPSIMD_ADDS = (3, 5, 7, 9, 11, 13, 15)
+GAINS_AT_START = 5
+GAINS_AFTER_ADD = {4: (5, 6), 6: (7, 8), 8: (9, 10), 10: (11, 12), 12: (13, 14), 14: (15,)}
+
+
+def tile_fluxattention_pa_t_kernel(
+    tc,
+    hidden_states,
+    encoder_hidden_states,
+    image_rotary_emb,
+    W_iqkv,
+    W_eqkv,
+    qn_scale,
+    kn_scale,
+    eqn_scale,
+    ekn_scale,
+    out_0,
+    out_1,
+    out_2,
+):
+    nc = tc.nc
+    x_img = hidden_states.flatten_outer_dims()
+    x_txt = encoder_hidden_states.flatten_outer_dims()
+    rot = image_rotary_emb.rearrange("l i f -> l (i f)")
+    outs = [out_0.flatten_outer_dims(), out_1.flatten_outer_dims(), out_2.flatten_outer_dims()]
+
+    n_units = len(UNIT_TILES)
+    first_tile = [sum(UNIT_TILES[:u]) for u in range(n_units)]
+
+    with ExitStack() as ctx:
+        ctx.enter_context(tc.manual_schedule())
+        const = ctx.enter_context(tc.tile_pool(name="const", bufs=1))
+        xpool4 = ctx.enter_context(tc.tile_pool(name="xpool4", bufs=sum(1 for nt in UNIT_TILES if nt == 4)))
+        xpool2 = ctx.enter_context(tc.tile_pool(name="xpool2", bufs=sum(1 for nt in UNIT_TILES if nt == 2)))
+        fpool = ctx.enter_context(tc.tile_pool(name="fpool", bufs=N_GROUPS))
+        fgpool = ctx.enter_context(tc.tile_pool(name="fgpool", bufs=N_GROUPS))
+        gpool = ctx.enter_context(tc.tile_pool(name="gpool", bufs=3))
+        cpool = ctx.enter_context(tc.tile_pool(name="cpool", bufs=3))
+        ppool = ctx.enter_context(tc.tile_pool(name="ppool", bufs=3))
+        opool = ctx.enter_context(tc.tile_pool(name="opool", bufs=4))
+        stat = ctx.enter_context(tc.tile_pool(name="stat", bufs=4))
+        tpsum = ctx.enter_context(tc.psum_pool(name="tpsum", bufs=2))
+        qkpsum = ctx.enter_context(tc.psum_pool(name="qkpsum", bufs=4))
+        vpsum = ctx.enter_context(tc.psum_pool(name="vpsum", bufs=2))
+
+        def group_rows(dram, u):
+            grp, t0 = divmod(first_tile[u], GROUP_TILES)
+            return dram[1024 * grp : 1024 * grp + 1024, :].rearrange("(p t) f -> p t f", t=GROUP_TILES)[
+                :, t0 : t0 + UNIT_TILES[u], :
+            ]
+
+        def load_gain(g, name):
+            raw = const.tile([P, 64], BF16, name=name + "_raw")
+            nc.scalar.dma_start(out=raw[:], in_=g.partition_broadcast(P))
+            return raw
+
+        def load_w(w, name):
+            raw = const.tile([P, 4, 384], BF16, name=name + "_raw")
+            for half in range(2):
+                nc.sync.dma_start(
+                    out=raw[:, 2 * half : 2 * half + 2, :],
+                    in_=w[256 * half : 256 * half + 256, :].rearrange("(p e) c -> p e c", e=2),
+                )
+            return raw
+
+        def load_x(u):
+            grp, t0 = divmod(first_tile[u], GROUP_TILES)
+            if grp < TEXT_GROUPS:
+                rows = x_txt[1024 * grp : 1024 * grp + 1024, :]
+            else:
+                rows = x_img[1024 * (grp - TEXT_GROUPS) : 1024 * (grp - TEXT_GROUPS) + 1024, :]
+            xpool = xpool4 if UNIT_TILES[u] == 4 else xpool2
+            xt = xpool.tile([P, UNIT_TILES[u], 512], BF16, name="x")
+            nc.sync.dma_start(
+                out=xt[:],
+                in_=rows.rearrange("(p t) k -> p t k", t=GROUP_TILES)[:, t0 : t0 + UNIT_TILES[u], :],
+            )
+            return xt
+
+        def load_f(grp):
+            ft = fpool.tile([P, GROUP_TILES, 128], BF16, name="f")
+            nc.sync.dma_start(
+                out=ft[:],
+                in_=rot[1024 * grp : 1024 * grp + 1024, :].rearrange("(p t) f -> p t f", t=GROUP_TILES),
+            )
+            return ft
+
+        g_raw = [
+            [load_gain(eqn_scale, "eq"), load_gain(ekn_scale, "ek")],
+            [load_gain(qn_scale, "iq"), load_gain(kn_scale, "ik")],
+        ]
+        x_tiles = {}
+        f_tiles = {}
+        w_raw = {}
+        x_tiles[0] = load_x(0)
+        w_raw[0] = load_w(W_eqkv, "we")
+        f_tiles[0] = load_f(0)
+        x_tiles[1] = load_x(1)
+        x_tiles[2] = load_x(2)
+        w_raw[1] = load_w(W_iqkv, "wi")
+        f_tiles[1] = load_f(1)
+        for u in range(3, n_units):
+            x_tiles[u] = load_x(u)
+            grp = u - 1
+            if grp < N_GROUPS:
+                f_tiles[grp] = load_f(grp)
+
+        ident = const.tile([P, P], F32, name="ident")
+        make_identity(nc, ident[:])
+        warm = const.tile([P, 1], F32, name="warm")
+        nc.vector.memset(warm[:], 1.0)
+        nc.scalar.activation(out=warm[:], in_=warm[:], func=ACT.Abs_reciprocal_sqrt)
+        junk = const.tile([P, 64], F32, name="junk")
+
+        def quantise_w(raw, name):
+            grouped = const.tile([P, 384, 4], BF16, name=name + "_grouped", align_bytes=64)
+            for b in range(2):
+                nc.vector.tensor_copy(
+                    out=grouped[:, 0:256, :].rearrange("p (g b i) t -> p g b i t", g=4, b=2, i=32)[:, :, b],
+                    in_=raw[:, :, 0:256].rearrange("p t (g i b) -> p g b i t", g=4, i=32, b=2)[:, :, b],
+                )
+            nc.vector.tensor_copy(
+                out=grouped[:, 256:384, :], in_=raw[:, :, 256:384].rearrange("p t n -> p n t")
+            )
+            codes = const.tile([P, 384], U32, name=name + "_codes", align_bytes=64)
+            scales = const.tile([P, 384], U8, name=name + "_scales", align_bytes=64)
+            for lo, hi in ((0, 256), (256, 384)):
+                nc.vector.quantize_mx(
+                    out=codes[:, lo:hi].bitcast(FP8X4),
+                    scales=scales[:, lo:hi],
+                    in_=grouped[:, lo:hi, :].rearrange("p n t -> p (n t)"),
+                )
+            return codes, scales
+
+        def expand_gain(raw, name):
+            gx = const.tile([P, 2, 32, 2], BF16, name=name + "_gx")
+            nc.vector.tensor_copy(
+                out=gx[:],
+                in_=raw[:].rearrange("p (i b) -> p b i", b=2).unsqueeze(3).to_broadcast([P, 2, 32, 2]),
+            )
+            return gx
+
+        fg_tiles = {}
+
+        def gain_rotary(k):
+            grp, q = divmod(k, 2)
+            if grp >= N_GROUPS:
+                return
+            s = 0 if grp < TEXT_GROUPS else 1
+            if q == 0:
+                fg_new = fgpool.tile([P, GROUP_TILES, 2, 128], F32, name="fg")
+                fg_tiles[grp] = fg_new
+            nc.gpsimd.tensor_tensor(
+                out=fg_tiles[grp][:, :, q, :].rearrange("p n (b c) -> p n b c", b=2),
+                in0=f_tiles[grp][:].rearrange("p n (c b) -> p n b c", b=2),
+                in1=g_x[s][q][:]
+                .rearrange("p b i a -> p b (i a)")
+                .unsqueeze(1)
+                .to_broadcast([P, GROUP_TILES, 2, 64]),
+                op=ALU.mult,
+            )
+
+        xt_tiles = {}
+        xg_tiles = {}
+        xq_tiles = {}
+        qk_tiles = {}
+        v_tiles = {}
+        rstd_tiles = {}
+        prod_tiles = {}
+
+        def valid(u):
+            return 0 <= u < n_units
+
+        def stage_transpose(u):
+            if not valid(u):
+                return
+            xw = x_tiles[u][:].bitcast(F32)
+            xt_tiles[u] = []
+            for j in range(UNIT_TILES[u] // 2):
+                xt = tpsum.tile([P, 2, 2, 128], F32, name="xt")
+                xt_tiles[u].append(xt)
+                for a in range(2):
+                    for half in range(2):
+                        nc.tensor.transpose(
+                            xt[:, a, half, :], xw[:, 2 * j + a, 128 * half : 128 * half + 128], ident[:]
+                        )
+
+        def stage_copy(u):
+            if not valid(u):
+                return
+            nb = UNIT_TILES[u] // 2
+            xg = gpool.tile([P, 512 * UNIT_TILES[u]], BF16, name="xg", align_bytes=64)
+            xg_tiles[u] = xg
+            xgw = xg[:].bitcast(F32).rearrange("p (j a r h) -> p j a r h", j=nb, a=2, r=128, h=2)
+            for j in range(nb):
+                nc.scalar.copy(out=xgw[:, j], in_=xt_tiles[u][j][:].rearrange("p a h r -> p a r h"))
+
+        def stage_quantise(u):
+            if not valid(u):
+                return
+            xc = cpool.tile([P, 128 * UNIT_TILES[u]], U32, name="xc", align_bytes=64)
+            xs = cpool.tile([P, 128 * UNIT_TILES[u]], U8, name="xs", align_bytes=64)
+            nc.vector.quantize_mx(out=xc[:].bitcast(FP8X4), scales=xs[:], in_=xg_tiles[u][:])
+            xq_tiles[u] = (xc, xs)
+
+        def stage_matmul(u):
+            if not valid(u):
+                return
+            s = 0 if first_tile[u] < TEXT_GROUPS * GROUP_TILES else 1
+            wc, ws = w_q[s]
+            xc, xs = xq_tiles[u]
+            vps = vpsum.tile([P, UNIT_TILES[u], 128], F32, name="vps")
+            v_tiles[u] = vps
+            qk_tiles[u] = []
+            for j in range(UNIT_TILES[u] // 2):
+                qk = qkpsum.tile([P, 2, 256], F32, name="qk")
+                qk_tiles[u].append(qk)
+                for a in range(2):
+                    t = 2 * j + a
+                    cols = slice(128 * t, 128 * t + 128)
+                    nc.tensor.matmul_mx(
+                        out=qk[:, a, :],
+                        lhsT=xc[:, cols].bitcast(FP8X4),
+                        lhsT_scale=xs[:, cols],
+                        rhs=wc[:, 0:256].bitcast(FP8X4),
+                        rhs_scale=ws[:, 0:256],
+                        start=True,
+                        stop=True,
+                    )
+                    nc.tensor.matmul_mx(
+                        out=vps[:, t, :],
+                        lhsT=xc[:, cols].bitcast(FP8X4),
+                        lhsT_scale=xs[:, cols],
+                        rhs=wc[:, 256:384].bitcast(FP8X4),
+                        rhs_scale=ws[:, 256:384],
+                        start=True,
+                        stop=True,
+                    )
+
+        def stage_stats(u):
+            if not valid(u):
+                return
+            nt = UNIT_TILES[u]
+            ssq = stat.tile([P, 4 * nt], F32, name="ssq")
+            for t in range(nt):
+                for g in range(4):
+                    nc.scalar.activation(
+                        out=junk[:],
+                        in_=qk_tiles[u][t // 2][:, t % 2, 64 * g : 64 * g + 64],
+                        func=ACT.Square,
+                        accum_out=ssq[:, 4 * t + g : 4 * t + g + 1],
+                    )
+            rstd = stat.tile([P, 4 * nt], F32, name="rstd")
+            nc.scalar.activation(
+                out=rstd[:], in_=ssq[:], func=ACT.Abs_reciprocal_sqrt, scale=1.0 / 64.0, bias=EPS
+            )
+            rstd_tiles[u] = rstd
+            vsb = opool.tile([P, nt, 128], F32, name="vsb")
+            nc.scalar.copy(out=vsb[:], in_=v_tiles[u][:])
+            nc.sync.dma_start(out=group_rows(outs[2], u), in_=vsb[:])
+
+        def stage_products(u):
+            if not valid(u):
+                return
+            nt = UNIT_TILES[u]
+            grp, t0 = divmod(first_tile[u], GROUP_TILES)
+            prod = ppool.tile([P, 2, nt, 2, 128], F32, name="prod")
+            prod_tiles[u] = prod
+            for t in range(nt):
+                for g in range(4):
+                    q, h = divmod(g, 2)
+                    nc.vector.scalar_tensor_tensor(
+                        out=prod[:, q, t, h, :].rearrange("p (c a) -> p c a", a=2),
+                        in0=qk_tiles[u][t // 2][:, t % 2, 64 * g : 64 * g + 64]
+                        .unsqueeze(2)
+                        .to_broadcast([P, 64, 2]),
+                        scalar=rstd_tiles[u][:, 4 * t + g : 4 * t + g + 1],
+                        in1=fg_tiles[grp][:, t0 + t, q, :].rearrange("p (c a) -> p c a", a=2),
+                        op0=ALU.mult,
+                        op1=ALU.mult,
+                    )
+
+        def stage_add(u):
+            if not valid(u):
+                return
+            nt = UNIT_TILES[u]
+            o = opool.tile([P, 2, nt, 128], F32, name="o")
+            pv = prod_tiles[u][:].rearrange("p q t h (b c) -> p (q t h) b c", b=2)
+            eng = nc.gpsimd if u in GPSIMD_ADDS else nc.vector
+            eng.tensor_tensor(
+                out=o[:].rearrange("p q t (h c) -> p (q t h) c", h=2),
+                in0=pv[:, :, 0, :],
+                in1=pv[:, :, 1, :],
+                op=ALU.add,
+            )
+            nc.sync.dma_start(out=group_rows(outs[0], u), in_=o[:, 0])
+            nc.sync.dma_start(out=group_rows(outs[1], u), in_=o[:, 1])
+
+        g_x = [
+            [expand_gain(g_raw[0][0], "eq"), expand_gain(g_raw[0][1], "ek")],
+            [expand_gain(g_raw[1][0], "iq"), expand_gain(g_raw[1][1], "ik")],
+        ]
+        w_q = {}
+        w_q[0] = quantise_w(w_raw[0], "we")
+        for k in range(GAINS_AT_START):
+            gain_rotary(k)
+        for i in range(-2, n_units + 2):
+            stage_copy(i + 1)
+            stage_transpose(i + 2)
+            stage_products(i - 1)
+            stage_quantise(i + 1)
+            stage_matmul(i + 1)
+            if i == -1:
+                w_q[1] = quantise_w(w_raw[1], "wi")
+            stage_stats(i)
+            stage_add(i - 1)
+            for k in GAINS_AFTER_ADD.get(i, ()):
+                gain_rotary(k)

@@ -19,9 +19,7 @@ GROUP_TILES = 8
 N_GROUPS = 8
 TEXT_GROUPS = 2
 UNIT_TILES = (2, 2, 4, 4, 4, 4, 4, 4, 4, 4, 4, 4, 4, 4, 4, 4, 2, 2)
-GPSIMD_ADDS = (3, 5, 7, 9, 11, 13, 15)
-GAINS_AT_START = 5
-GAINS_AFTER_ADD = {4: (5, 6), 6: (7, 8), 8: (9, 10), 10: (11, 12), 12: (13, 14), 14: (15,)}
+GPSIMD_ADDS = ()
 
 
 def tile_fluxattention_pa_t_kernel(
@@ -113,8 +111,8 @@ def tile_fluxattention_pa_t_kernel(
         x_tiles = {}
         f_tiles = {}
         w_raw = {}
-        x_tiles[0] = load_x(0)
         w_raw[0] = load_w(W_eqkv, "we")
+        x_tiles[0] = load_x(0)
         f_tiles[0] = load_f(0)
         x_tiles[1] = load_x(1)
         x_tiles[2] = load_x(2)
@@ -133,16 +131,17 @@ def tile_fluxattention_pa_t_kernel(
         nc.scalar.activation(out=warm[:], in_=warm[:], func=ACT.Abs_reciprocal_sqrt)
         junk = const.tile([P, 64], F32, name="junk")
 
-        def quantise_w(raw, name):
+        def regroup_w(raw, name, copy):
             grouped = const.tile([P, 384, 4], BF16, name=name + "_grouped", align_bytes=64)
             for b in range(2):
-                nc.vector.tensor_copy(
+                copy(
                     out=grouped[:, 0:256, :].rearrange("p (g b i) t -> p g b i t", g=4, b=2, i=32)[:, :, b],
                     in_=raw[:, :, 0:256].rearrange("p t (g i b) -> p g b i t", g=4, i=32, b=2)[:, :, b],
                 )
-            nc.vector.tensor_copy(
-                out=grouped[:, 256:384, :], in_=raw[:, :, 256:384].rearrange("p t n -> p n t")
-            )
+            copy(out=grouped[:, 256:384, :], in_=raw[:, :, 256:384].rearrange("p t n -> p n t"))
+            return grouped
+
+        def quantise_w(grouped, name):
             codes = const.tile([P, 384], U32, name=name + "_codes", align_bytes=64)
             scales = const.tile([P, 384], U8, name=name + "_scales", align_bytes=64)
             for lo, hi in ((0, 256), (256, 384)):
@@ -171,7 +170,7 @@ def tile_fluxattention_pa_t_kernel(
             if q == 0:
                 fg_new = fgpool.tile([P, GROUP_TILES, 2, 128], F32, name="fg")
                 fg_tiles[grp] = fg_new
-            nc.gpsimd.tensor_tensor(
+            nc.vector.tensor_tensor(
                 out=fg_tiles[grp][:, :, q, :].rearrange("p n (b c) -> p n b c", b=2),
                 in0=f_tiles[grp][:].rearrange("p n (c b) -> p n b c", b=2),
                 in1=g_x[s][q][:]
@@ -322,18 +321,25 @@ def tile_fluxattention_pa_t_kernel(
             [expand_gain(g_raw[1][0], "iq"), expand_gain(g_raw[1][1], "ik")],
         ]
         w_q = {}
-        w_q[0] = quantise_w(w_raw[0], "we")
-        for k in range(GAINS_AT_START):
-            gain_rotary(k)
+        w_q[0] = quantise_w(regroup_w(w_raw[0], "we", nc.vector.tensor_copy), "we")
+        w_grouped = {}
         for i in range(-2, n_units + 2):
             stage_copy(i + 1)
             stage_transpose(i + 2)
             stage_products(i - 1)
             stage_quantise(i + 1)
             stage_matmul(i + 1)
-            if i == -1:
-                w_q[1] = quantise_w(w_raw[1], "wi")
             stage_stats(i)
             stage_add(i - 1)
-            for k in GAINS_AFTER_ADD.get(i, ()):
-                gain_rotary(k)
+            if i == 0:
+                w_grouped[1] = regroup_w(w_raw[1], "wi", nc.scalar.copy)
+            if i == 1:
+                w_q[1] = quantise_w(w_grouped[1], "wi")
+            if i == -1:
+                gain_rotary(0)
+                gain_rotary(1)
+            elif i == 0:
+                gain_rotary(2)
+                gain_rotary(3)
+            elif i >= 1:
+                gain_rotary(i + 3)

@@ -19,7 +19,9 @@ GROUP_TILES = 8
 N_GROUPS = 8
 TEXT_GROUPS = 2
 UNIT_TILES = (2, 2, 4, 4, 4, 4, 4, 4, 4, 4, 4, 4, 4, 4, 4, 4, 2, 2)
-GPSIMD_ADDS = ()
+GPSIMD_ADDS = (3, 5, 7, 9, 11, 13, 15)
+GAINS_AT_START = 5
+GAINS_AFTER_ADD = {4: (5, 6), 6: (7, 8), 8: (9, 10), 10: (11, 12), 12: (13, 14), 14: (15,)}
 
 
 def tile_fluxattention_pa_t_kernel(
@@ -52,7 +54,8 @@ def tile_fluxattention_pa_t_kernel(
         xpool4 = ctx.enter_context(tc.tile_pool(name="xpool4", bufs=sum(1 for nt in UNIT_TILES if nt == 4)))
         xpool2 = ctx.enter_context(tc.tile_pool(name="xpool2", bufs=sum(1 for nt in UNIT_TILES if nt == 2)))
         fpool = ctx.enter_context(tc.tile_pool(name="fpool", bufs=N_GROUPS))
-        fgpool = ctx.enter_context(tc.tile_pool(name="fgpool", bufs=N_GROUPS))
+        fgpool = ctx.enter_context(tc.tile_pool(name="fgpool", bufs=4))
+        sqpool = ctx.enter_context(tc.tile_pool(name="sqpool", bufs=2))
         gpool = ctx.enter_context(tc.tile_pool(name="gpool", bufs=3))
         cpool = ctx.enter_context(tc.tile_pool(name="cpool", bufs=3))
         ppool = ctx.enter_context(tc.tile_pool(name="ppool", bufs=3))
@@ -129,7 +132,6 @@ def tile_fluxattention_pa_t_kernel(
         warm = const.tile([P, 1], F32, name="warm")
         nc.vector.memset(warm[:], 1.0)
         nc.scalar.activation(out=warm[:], in_=warm[:], func=ACT.Abs_reciprocal_sqrt)
-        junk = const.tile([P, 64], F32, name="junk")
 
         def regroup_w(raw, name, copy):
             grouped = const.tile([P, 384, 4], BF16, name=name + "_grouped", align_bytes=64)
@@ -170,7 +172,7 @@ def tile_fluxattention_pa_t_kernel(
             if q == 0:
                 fg_new = fgpool.tile([P, GROUP_TILES, 2, 128], F32, name="fg")
                 fg_tiles[grp] = fg_new
-            nc.vector.tensor_tensor(
+            nc.gpsimd.tensor_tensor(
                 out=fg_tiles[grp][:, :, q, :].rearrange("p n (b c) -> p n b c", b=2),
                 in0=f_tiles[grp][:].rearrange("p n (c b) -> p n b c", b=2),
                 in1=g_x[s][q][:]
@@ -186,6 +188,8 @@ def tile_fluxattention_pa_t_kernel(
         qk_tiles = {}
         v_tiles = {}
         rstd_tiles = {}
+        sq_tiles = {}
+        ssq_tiles = {}
         prod_tiles = {}
 
         def valid(u):
@@ -257,27 +261,42 @@ def tile_fluxattention_pa_t_kernel(
                         stop=True,
                     )
 
-        def stage_stats(u):
+        def stage_square(u):
+            if not valid(u):
+                return
+            sq = sqpool.tile([P, 256 * UNIT_TILES[u]], F32, name="sq")
+            sq_tiles[u] = sq
+            for j in range(UNIT_TILES[u] // 2):
+                nc.scalar.activation(
+                    out=sq[:, 512 * j : 512 * j + 512],
+                    in_=qk_tiles[u][j][:].rearrange("p a c -> p (a c)"),
+                    func=ACT.Square,
+                )
+
+        def stage_reduce(u):
+            if not valid(u):
+                return
+            ssq = stat.tile([P, 4 * UNIT_TILES[u]], F32, name="ssq")
+            ssq_tiles[u] = ssq
+            nc.vector.tensor_reduce(
+                out=ssq[:],
+                in_=sq_tiles[u][:].rearrange("p (g c) -> p g c", c=64),
+                axis=mybir.AxisListType.X,
+                op=ALU.add,
+            )
+
+        def stage_rstd(u):
             if not valid(u):
                 return
             nt = UNIT_TILES[u]
-            ssq = stat.tile([P, 4 * nt], F32, name="ssq")
-            for t in range(nt):
-                for g in range(4):
-                    nc.scalar.activation(
-                        out=junk[:],
-                        in_=qk_tiles[u][t // 2][:, t % 2, 64 * g : 64 * g + 64],
-                        func=ACT.Square,
-                        accum_out=ssq[:, 4 * t + g : 4 * t + g + 1],
-                    )
-            rstd = stat.tile([P, 4 * nt], F32, name="rstd")
-            nc.scalar.activation(
-                out=rstd[:], in_=ssq[:], func=ACT.Abs_reciprocal_sqrt, scale=1.0 / 64.0, bias=EPS
-            )
-            rstd_tiles[u] = rstd
             vsb = opool.tile([P, nt, 128], F32, name="vsb")
             nc.scalar.copy(out=vsb[:], in_=v_tiles[u][:])
             nc.sync.dma_start(out=group_rows(outs[2], u), in_=vsb[:])
+            rstd = stat.tile([P, 4 * nt], F32, name="rstd")
+            nc.scalar.activation(
+                out=rstd[:], in_=ssq_tiles[u][:], func=ACT.Abs_reciprocal_sqrt, scale=1.0 / 64.0, bias=EPS
+            )
+            rstd_tiles[u] = rstd
 
         def stage_products(u):
             if not valid(u):
@@ -323,23 +342,21 @@ def tile_fluxattention_pa_t_kernel(
         w_q = {}
         w_q[0] = quantise_w(regroup_w(w_raw[0], "we", nc.vector.tensor_copy), "we")
         w_grouped = {}
+        for k in range(GAINS_AT_START):
+            gain_rotary(k)
         for i in range(-2, n_units + 2):
             stage_copy(i + 1)
             stage_transpose(i + 2)
+            stage_square(i)
             stage_products(i - 1)
+            stage_reduce(i)
             stage_quantise(i + 1)
             stage_matmul(i + 1)
-            stage_stats(i)
+            stage_rstd(i)
             stage_add(i - 1)
             if i == 0:
                 w_grouped[1] = regroup_w(w_raw[1], "wi", nc.scalar.copy)
             if i == 1:
                 w_q[1] = quantise_w(w_grouped[1], "wi")
-            if i == -1:
-                gain_rotary(0)
-                gain_rotary(1)
-            elif i == 0:
-                gain_rotary(2)
-                gain_rotary(3)
-            elif i >= 1:
-                gain_rotary(i + 3)
+            for k in GAINS_AFTER_ADD.get(i, ()):
+                gain_rotary(k)

@@ -18,10 +18,12 @@ EPS = 1e-6
 GROUP_TILES = 8
 N_GROUPS = 8
 TEXT_GROUPS = 2
-UNIT_TILES = (2, 2, 4, 4, 4, 4, 4, 4, 4, 4, 4, 4, 4, 4, 4, 4, 2, 2)
-GPSIMD_ADDS = (3, 5, 7, 9, 11, 13, 15)
+UNIT_TILES = 2
+N_UNITS = 32
+CHUNK_TILES = 4
+N_CHUNKS = 16
+GPSIMD_ADDS = (5, 7, 9, 10, 11, 13, 15, 16, 17, 19, 21, 22, 23, 25, 27, 29)
 GAINS_AT_START = 5
-GAINS_AFTER_ADD = {4: (5, 6), 6: (7, 8), 8: (9, 10), 10: (11, 12), 12: (13, 14), 14: (15,)}
 
 
 def tile_fluxattention_pa_t_kernel(
@@ -45,30 +47,26 @@ def tile_fluxattention_pa_t_kernel(
     rot = image_rotary_emb.rearrange("l i f -> l (i f)")
     outs = [out_0.flatten_outer_dims(), out_1.flatten_outer_dims(), out_2.flatten_outer_dims()]
 
-    n_units = len(UNIT_TILES)
-    first_tile = [sum(UNIT_TILES[:u]) for u in range(n_units)]
-
     with ExitStack() as ctx:
         ctx.enter_context(tc.manual_schedule())
         const = ctx.enter_context(tc.tile_pool(name="const", bufs=1))
-        xpool4 = ctx.enter_context(tc.tile_pool(name="xpool4", bufs=sum(1 for nt in UNIT_TILES if nt == 4)))
-        xpool2 = ctx.enter_context(tc.tile_pool(name="xpool2", bufs=sum(1 for nt in UNIT_TILES if nt == 2)))
+        xpool = ctx.enter_context(tc.tile_pool(name="xpool", bufs=N_CHUNKS))
         fpool = ctx.enter_context(tc.tile_pool(name="fpool", bufs=N_GROUPS))
         fgpool = ctx.enter_context(tc.tile_pool(name="fgpool", bufs=4))
-        sqpool = ctx.enter_context(tc.tile_pool(name="sqpool", bufs=2))
+        sqpool = ctx.enter_context(tc.tile_pool(name="sqpool", bufs=3))
         gpool = ctx.enter_context(tc.tile_pool(name="gpool", bufs=3))
         cpool = ctx.enter_context(tc.tile_pool(name="cpool", bufs=3))
-        ppool = ctx.enter_context(tc.tile_pool(name="ppool", bufs=3))
+        ppool = ctx.enter_context(tc.tile_pool(name="ppool", bufs=4))
         opool = ctx.enter_context(tc.tile_pool(name="opool", bufs=4))
         stat = ctx.enter_context(tc.tile_pool(name="stat", bufs=4))
         tpsum = ctx.enter_context(tc.psum_pool(name="tpsum", bufs=2))
         qkpsum = ctx.enter_context(tc.psum_pool(name="qkpsum", bufs=4))
         vpsum = ctx.enter_context(tc.psum_pool(name="vpsum", bufs=2))
 
-        def group_rows(dram, u):
-            grp, t0 = divmod(first_tile[u], GROUP_TILES)
+        def chunk_rows(dram, c, lo, hi):
+            grp, half = divmod(c, 2)
             return dram[1024 * grp : 1024 * grp + 1024, :].rearrange("(p t) f -> p t f", t=GROUP_TILES)[
-                :, t0 : t0 + UNIT_TILES[u], :
+                :, 4 * half + lo : 4 * half + hi, :
             ]
 
         def load_gain(g, name):
@@ -85,18 +83,17 @@ def tile_fluxattention_pa_t_kernel(
                 )
             return raw
 
-        def load_x(u):
-            grp, t0 = divmod(first_tile[u], GROUP_TILES)
-            if grp < TEXT_GROUPS:
-                rows = x_txt[1024 * grp : 1024 * grp + 1024, :]
+        def load_x(c, pieces):
+            if c < 2 * TEXT_GROUPS:
+                src, cc = x_txt, c
             else:
-                rows = x_img[1024 * (grp - TEXT_GROUPS) : 1024 * (grp - TEXT_GROUPS) + 1024, :]
-            xpool = xpool4 if UNIT_TILES[u] == 4 else xpool2
-            xt = xpool.tile([P, UNIT_TILES[u], 512], BF16, name="x")
-            nc.sync.dma_start(
-                out=xt[:],
-                in_=rows.rearrange("(p t) k -> p t k", t=GROUP_TILES)[:, t0 : t0 + UNIT_TILES[u], :],
-            )
+                src, cc = x_img, c - 2 * TEXT_GROUPS
+            xt = xpool.tile([P, CHUNK_TILES, 512], BF16, name="x")
+            step = CHUNK_TILES // pieces
+            for k in range(pieces):
+                nc.sync.dma_start(
+                    out=xt[:, step * k : step * k + step, :], in_=chunk_rows(src, cc, step * k, step * k + step)
+                )
             return xt
 
         def load_f(grp):
@@ -115,17 +112,15 @@ def tile_fluxattention_pa_t_kernel(
         f_tiles = {}
         w_raw = {}
         w_raw[0] = load_w(W_eqkv, "we")
-        x_tiles[0] = load_x(0)
+        x_tiles[0] = load_x(0, 2)
         f_tiles[0] = load_f(0)
-        x_tiles[1] = load_x(1)
-        x_tiles[2] = load_x(2)
+        x_tiles[1] = load_x(1, 1)
         w_raw[1] = load_w(W_iqkv, "wi")
         f_tiles[1] = load_f(1)
-        for u in range(3, n_units):
-            x_tiles[u] = load_x(u)
-            grp = u - 1
-            if grp < N_GROUPS:
-                f_tiles[grp] = load_f(grp)
+        for c in range(2, N_CHUNKS):
+            x_tiles[c] = load_x(c, 1)
+            if c < N_GROUPS:
+                f_tiles[c] = load_f(c)
 
         ident = const.tile([P, P], F32, name="ident")
         make_identity(nc, ident[:])
@@ -166,8 +161,6 @@ def tile_fluxattention_pa_t_kernel(
 
         def gain_rotary(k):
             grp, q = divmod(k, 2)
-            if grp >= N_GROUPS:
-                return
             s = 0 if grp < TEXT_GROUPS else 1
             if q == 0:
                 fg_new = fgpool.tile([P, GROUP_TILES, 2, 128], F32, name="fg")
@@ -187,96 +180,98 @@ def tile_fluxattention_pa_t_kernel(
         xq_tiles = {}
         qk_tiles = {}
         v_tiles = {}
-        rstd_tiles = {}
         sq_tiles = {}
         ssq_tiles = {}
+        rstd_tiles = {}
         prod_tiles = {}
+        o_tiles = {}
+        vsb_tiles = {}
 
         def valid(u):
-            return 0 <= u < n_units
+            return 0 <= u < N_UNITS
 
         def stage_transpose(u):
             if not valid(u):
                 return
-            xw = x_tiles[u][:].bitcast(F32)
-            xt_tiles[u] = []
-            for j in range(UNIT_TILES[u] // 2):
-                xt = tpsum.tile([P, 2, 2, 128], F32, name="xt")
-                xt_tiles[u].append(xt)
-                for a in range(2):
-                    for half in range(2):
-                        nc.tensor.transpose(
-                            xt[:, a, half, :], xw[:, 2 * j + a, 128 * half : 128 * half + 128], ident[:]
-                        )
+            xw = x_tiles[u // 2][:].bitcast(F32)
+            xt = tpsum.tile([P, 2, 2, 128], F32, name="xt")
+            xt_tiles[u] = xt
+            for a in range(2):
+                for half in range(2):
+                    nc.tensor.transpose(
+                        xt[:, a, half, :], xw[:, 2 * (u % 2) + a, 128 * half : 128 * half + 128], ident[:]
+                    )
 
         def stage_copy(u):
             if not valid(u):
                 return
-            nb = UNIT_TILES[u] // 2
-            xg = gpool.tile([P, 512 * UNIT_TILES[u]], BF16, name="xg", align_bytes=64)
+            xg = gpool.tile([P, 1024], BF16, name="xg", align_bytes=64)
             xg_tiles[u] = xg
-            xgw = xg[:].bitcast(F32).rearrange("p (j a r h) -> p j a r h", j=nb, a=2, r=128, h=2)
-            for j in range(nb):
-                nc.scalar.copy(out=xgw[:, j], in_=xt_tiles[u][j][:].rearrange("p a h r -> p a r h"))
+            nc.scalar.copy(
+                out=xg[:].bitcast(F32).rearrange("p (a r h) -> p a r h", a=2, r=128, h=2),
+                in_=xt_tiles[u][:].rearrange("p a h r -> p a r h"),
+            )
 
         def stage_quantise(u):
             if not valid(u):
                 return
-            xc = cpool.tile([P, 128 * UNIT_TILES[u]], U32, name="xc", align_bytes=64)
-            xs = cpool.tile([P, 128 * UNIT_TILES[u]], U8, name="xs", align_bytes=64)
+            xc = cpool.tile([P, 256], U32, name="xc", align_bytes=64)
+            xs = cpool.tile([P, 256], U8, name="xs", align_bytes=64)
             nc.vector.quantize_mx(out=xc[:].bitcast(FP8X4), scales=xs[:], in_=xg_tiles[u][:])
             xq_tiles[u] = (xc, xs)
 
         def stage_matmul(u):
             if not valid(u):
                 return
-            s = 0 if first_tile[u] < TEXT_GROUPS * GROUP_TILES else 1
-            wc, ws = w_q[s]
+            wc, ws = w_q[0 if u < 4 * TEXT_GROUPS else 1]
             xc, xs = xq_tiles[u]
-            vps = vpsum.tile([P, UNIT_TILES[u], 128], F32, name="vps")
+            vps = vpsum.tile([P, 2, 128], F32, name="vps")
             v_tiles[u] = vps
-            qk_tiles[u] = []
-            for j in range(UNIT_TILES[u] // 2):
-                qk = qkpsum.tile([P, 2, 256], F32, name="qk")
-                qk_tiles[u].append(qk)
-                for a in range(2):
-                    t = 2 * j + a
-                    cols = slice(128 * t, 128 * t + 128)
-                    nc.tensor.matmul_mx(
-                        out=qk[:, a, :],
-                        lhsT=xc[:, cols].bitcast(FP8X4),
-                        lhsT_scale=xs[:, cols],
-                        rhs=wc[:, 0:256].bitcast(FP8X4),
-                        rhs_scale=ws[:, 0:256],
-                        start=True,
-                        stop=True,
-                    )
-                    nc.tensor.matmul_mx(
-                        out=vps[:, t, :],
-                        lhsT=xc[:, cols].bitcast(FP8X4),
-                        lhsT_scale=xs[:, cols],
-                        rhs=wc[:, 256:384].bitcast(FP8X4),
-                        rhs_scale=ws[:, 256:384],
-                        start=True,
-                        stop=True,
-                    )
+            qk = qkpsum.tile([P, 2, 256], F32, name="qk")
+            qk_tiles[u] = qk
+            for a in range(2):
+                cols = slice(128 * a, 128 * a + 128)
+                nc.tensor.matmul_mx(
+                    out=qk[:, a, :],
+                    lhsT=xc[:, cols].bitcast(FP8X4),
+                    lhsT_scale=xs[:, cols],
+                    rhs=wc[:, 0:256].bitcast(FP8X4),
+                    rhs_scale=ws[:, 0:256],
+                    start=True,
+                    stop=True,
+                )
+                nc.tensor.matmul_mx(
+                    out=vps[:, a, :],
+                    lhsT=xc[:, cols].bitcast(FP8X4),
+                    lhsT_scale=xs[:, cols],
+                    rhs=wc[:, 256:384].bitcast(FP8X4),
+                    rhs_scale=ws[:, 256:384],
+                    start=True,
+                    stop=True,
+                )
 
         def stage_square(u):
             if not valid(u):
                 return
-            sq = sqpool.tile([P, 256 * UNIT_TILES[u]], F32, name="sq")
+            sq = sqpool.tile([P, 512], F32, name="sq")
             sq_tiles[u] = sq
-            for j in range(UNIT_TILES[u] // 2):
-                nc.scalar.activation(
-                    out=sq[:, 512 * j : 512 * j + 512],
-                    in_=qk_tiles[u][j][:].rearrange("p a c -> p (a c)"),
-                    func=ACT.Square,
-                )
+            nc.scalar.activation(out=sq[:], in_=qk_tiles[u][:].rearrange("p a c -> p (a c)"), func=ACT.Square)
+
+        def stage_v(u):
+            if not valid(u):
+                return
+            if u % 2 == 0:
+                vsb_new = opool.tile([P, CHUNK_TILES, 128], F32, name="vsb")
+                vsb_tiles[u // 2] = vsb_new
+            vsb = vsb_tiles[u // 2]
+            nc.scalar.copy(out=vsb[:, 2 * (u % 2) : 2 * (u % 2) + 2, :], in_=v_tiles[u][:])
+            if u % 2 == 1:
+                nc.sync.dma_start(out=chunk_rows(outs[2], u // 2, 0, CHUNK_TILES), in_=vsb[:])
 
         def stage_reduce(u):
             if not valid(u):
                 return
-            ssq = stat.tile([P, 4 * UNIT_TILES[u]], F32, name="ssq")
+            ssq = stat.tile([P, 8], F32, name="ssq")
             ssq_tiles[u] = ssq
             nc.vector.tensor_reduce(
                 out=ssq[:],
@@ -288,11 +283,7 @@ def tile_fluxattention_pa_t_kernel(
         def stage_rstd(u):
             if not valid(u):
                 return
-            nt = UNIT_TILES[u]
-            vsb = opool.tile([P, nt, 128], F32, name="vsb")
-            nc.scalar.copy(out=vsb[:], in_=v_tiles[u][:])
-            nc.sync.dma_start(out=group_rows(outs[2], u), in_=vsb[:])
-            rstd = stat.tile([P, 4 * nt], F32, name="rstd")
+            rstd = stat.tile([P, 8], F32, name="rstd")
             nc.scalar.activation(
                 out=rstd[:], in_=ssq_tiles[u][:], func=ACT.Abs_reciprocal_sqrt, scale=1.0 / 64.0, bias=EPS
             )
@@ -301,18 +292,15 @@ def tile_fluxattention_pa_t_kernel(
         def stage_products(u):
             if not valid(u):
                 return
-            nt = UNIT_TILES[u]
-            grp, t0 = divmod(first_tile[u], GROUP_TILES)
-            prod = ppool.tile([P, 2, nt, 2, 128], F32, name="prod")
+            grp, t0 = divmod(2 * u, GROUP_TILES)
+            prod = ppool.tile([P, 2, 2, 2, 128], F32, name="prod")
             prod_tiles[u] = prod
-            for t in range(nt):
+            for t in range(2):
                 for g in range(4):
                     q, h = divmod(g, 2)
                     nc.vector.scalar_tensor_tensor(
                         out=prod[:, q, t, h, :].rearrange("p (c a) -> p c a", a=2),
-                        in0=qk_tiles[u][t // 2][:, t % 2, 64 * g : 64 * g + 64]
-                        .unsqueeze(2)
-                        .to_broadcast([P, 64, 2]),
+                        in0=qk_tiles[u][:, t, 64 * g : 64 * g + 64].unsqueeze(2).to_broadcast([P, 64, 2]),
                         scalar=rstd_tiles[u][:, 4 * t + g : 4 * t + g + 1],
                         in1=fg_tiles[grp][:, t0 + t, q, :].rearrange("p (c a) -> p c a", a=2),
                         op0=ALU.mult,
@@ -322,18 +310,21 @@ def tile_fluxattention_pa_t_kernel(
         def stage_add(u):
             if not valid(u):
                 return
-            nt = UNIT_TILES[u]
-            o = opool.tile([P, 2, nt, 128], F32, name="o")
-            pv = prod_tiles[u][:].rearrange("p q t h (b c) -> p (q t h) b c", b=2)
+            if u % 2 == 0:
+                o_new = opool.tile([P, 2, CHUNK_TILES, 128], F32, name="o")
+                o_tiles[u // 2] = o_new
+            o = o_tiles[u // 2]
+            pv = prod_tiles[u][:].rearrange("p q t h (b c) -> p q (t h) b c", b=2)
             eng = nc.gpsimd if u in GPSIMD_ADDS else nc.vector
             eng.tensor_tensor(
-                out=o[:].rearrange("p q t (h c) -> p (q t h) c", h=2),
-                in0=pv[:, :, 0, :],
-                in1=pv[:, :, 1, :],
+                out=o[:, :, 2 * (u % 2) : 2 * (u % 2) + 2, :].rearrange("p q t (h c) -> p q (t h) c", h=2),
+                in0=pv[:, :, :, 0, :],
+                in1=pv[:, :, :, 1, :],
                 op=ALU.add,
             )
-            nc.sync.dma_start(out=group_rows(outs[0], u), in_=o[:, 0])
-            nc.sync.dma_start(out=group_rows(outs[1], u), in_=o[:, 1])
+            if u % 2 == 1:
+                nc.sync.dma_start(out=chunk_rows(outs[0], u // 2, 0, CHUNK_TILES), in_=o[:, 0])
+                nc.sync.dma_start(out=chunk_rows(outs[1], u // 2, 0, CHUNK_TILES), in_=o[:, 1])
 
         g_x = [
             [expand_gain(g_raw[0][0], "eq"), expand_gain(g_raw[0][1], "ek")],
@@ -344,19 +335,22 @@ def tile_fluxattention_pa_t_kernel(
         w_grouped = {}
         for k in range(GAINS_AT_START):
             gain_rotary(k)
-        for i in range(-2, n_units + 2):
-            stage_copy(i + 1)
-            stage_transpose(i + 2)
-            stage_square(i)
-            stage_products(i - 1)
-            stage_reduce(i)
-            stage_quantise(i + 1)
-            stage_matmul(i + 1)
+        for i in range(-5, N_UNITS + 2):
             stage_rstd(i)
+            stage_copy(i + 4)
+            stage_transpose(i + 5)
+            stage_square(i + 2)
+            stage_v(i + 2)
+            stage_products(i - 1)
+            stage_reduce(i + 1)
+            stage_quantise(i + 3)
+            stage_matmul(i + 3)
             stage_add(i - 1)
-            if i == 0:
-                w_grouped[1] = regroup_w(w_raw[1], "wi", nc.scalar.copy)
             if i == 1:
+                w_grouped[1] = regroup_w(w_raw[1], "wi", nc.scalar.copy)
+            if i == 3:
                 w_q[1] = quantise_w(w_grouped[1], "wi")
-            for k in GAINS_AFTER_ADD.get(i, ()):
-                gain_rotary(k)
+            if (i + 7) % 4 == 0 and GAINS_AT_START <= (i + 7) // 2 < 2 * N_GROUPS:
+                gain_rotary((i + 7) // 2)
+            if (i + 5) % 4 == 0 and GAINS_AT_START <= (i + 5) // 2 + 1 < 2 * N_GROUPS:
+                gain_rotary((i + 5) // 2 + 1)

@@ -22,8 +22,8 @@ UNIT_TILES = 2
 N_UNITS = 32
 CHUNK_TILES = 4
 N_CHUNKS = 16
-GPSIMD_ADDS = (5, 7, 9, 10, 11, 13, 15, 16, 17, 19, 21, 22, 23, 25, 27, 29)
-GAINS_AT_START = 5
+VECTOR_ADD_CHUNKS = (0, 2, 4, 6, 8, 10, 12, 14, 15)
+GAINS_AT_START = 8
 
 
 def tile_fluxattention_pa_t_kernel(
@@ -56,7 +56,7 @@ def tile_fluxattention_pa_t_kernel(
         sqpool = ctx.enter_context(tc.tile_pool(name="sqpool", bufs=3))
         gpool = ctx.enter_context(tc.tile_pool(name="gpool", bufs=3))
         cpool = ctx.enter_context(tc.tile_pool(name="cpool", bufs=3))
-        ppool = ctx.enter_context(tc.tile_pool(name="ppool", bufs=4))
+        ppool = ctx.enter_context(tc.tile_pool(name="ppool", bufs=3))
         opool = ctx.enter_context(tc.tile_pool(name="opool", bufs=4))
         stat = ctx.enter_context(tc.tile_pool(name="stat", bufs=4))
         tpsum = ctx.enter_context(tc.psum_pool(name="tpsum", bufs=2))
@@ -159,19 +159,21 @@ def tile_fluxattention_pa_t_kernel(
 
         fg_tiles = {}
 
-        def gain_rotary(k):
-            grp, q = divmod(k, 2)
+        def gain_rotary(m):
+            c, q = divmod(m, 2)
+            grp, half = divmod(c, 2)
             s = 0 if grp < TEXT_GROUPS else 1
-            if q == 0:
+            if m % 4 == 0:
                 fg_new = fgpool.tile([P, GROUP_TILES, 2, 128], F32, name="fg")
                 fg_tiles[grp] = fg_new
+            tiles = slice(4 * half, 4 * half + 4)
             nc.gpsimd.tensor_tensor(
-                out=fg_tiles[grp][:, :, q, :].rearrange("p n (b c) -> p n b c", b=2),
-                in0=f_tiles[grp][:].rearrange("p n (c b) -> p n b c", b=2),
+                out=fg_tiles[grp][:, tiles, q, :].rearrange("p n (b c) -> p n b c", b=2),
+                in0=f_tiles[grp][:, tiles, :].rearrange("p n (c b) -> p n b c", b=2),
                 in1=g_x[s][q][:]
                 .rearrange("p b i a -> p b (i a)")
                 .unsqueeze(1)
-                .to_broadcast([P, GROUP_TILES, 2, 64]),
+                .to_broadcast([P, CHUNK_TILES, 2, 64]),
                 op=ALU.mult,
             )
 
@@ -205,32 +207,36 @@ def tile_fluxattention_pa_t_kernel(
         def stage_copy(u):
             if not valid(u):
                 return
-            xg = gpool.tile([P, 1024], BF16, name="xg", align_bytes=64)
-            xg_tiles[u] = xg
+            if u % 2 == 0:
+                xg_new = gpool.tile([P, 2048], BF16, name="xg", align_bytes=64)
+                xg_tiles[u // 2] = xg_new
+            xg = xg_tiles[u // 2]
             nc.scalar.copy(
-                out=xg[:].bitcast(F32).rearrange("p (a r h) -> p a r h", a=2, r=128, h=2),
+                out=xg[:, 1024 * (u % 2) : 1024 * (u % 2) + 1024]
+                .bitcast(F32)
+                .rearrange("p (a r h) -> p a r h", a=2, r=128, h=2),
                 in_=xt_tiles[u][:].rearrange("p a h r -> p a r h"),
             )
 
-        def stage_quantise(u):
-            if not valid(u):
+        def stage_quantise(c):
+            if not 0 <= c < N_CHUNKS:
                 return
-            xc = cpool.tile([P, 256], U32, name="xc", align_bytes=64)
-            xs = cpool.tile([P, 256], U8, name="xs", align_bytes=64)
-            nc.vector.quantize_mx(out=xc[:].bitcast(FP8X4), scales=xs[:], in_=xg_tiles[u][:])
-            xq_tiles[u] = (xc, xs)
+            xc = cpool.tile([P, 512], U32, name="xc", align_bytes=64)
+            xs = cpool.tile([P, 512], U8, name="xs", align_bytes=64)
+            nc.vector.quantize_mx(out=xc[:].bitcast(FP8X4), scales=xs[:], in_=xg_tiles[c][:])
+            xq_tiles[c] = (xc, xs)
 
         def stage_matmul(u):
             if not valid(u):
                 return
             wc, ws = w_q[0 if u < 4 * TEXT_GROUPS else 1]
-            xc, xs = xq_tiles[u]
+            xc, xs = xq_tiles[u // 2]
             vps = vpsum.tile([P, 2, 128], F32, name="vps")
             v_tiles[u] = vps
             qk = qkpsum.tile([P, 2, 256], F32, name="qk")
             qk_tiles[u] = qk
             for a in range(2):
-                cols = slice(128 * a, 128 * a + 128)
+                cols = slice(256 * (u % 2) + 128 * a, 256 * (u % 2) + 128 * a + 128)
                 nc.tensor.matmul_mx(
                     out=qk[:, a, :],
                     lhsT=xc[:, cols].bitcast(FP8X4),
@@ -293,13 +299,15 @@ def tile_fluxattention_pa_t_kernel(
             if not valid(u):
                 return
             grp, t0 = divmod(2 * u, GROUP_TILES)
-            prod = ppool.tile([P, 2, 2, 2, 128], F32, name="prod")
-            prod_tiles[u] = prod
+            if u % 2 == 0:
+                prod_new = ppool.tile([P, 2, CHUNK_TILES, 2, 128], F32, name="prod")
+                prod_tiles[u // 2] = prod_new
+            prod = prod_tiles[u // 2]
             for t in range(2):
                 for g in range(4):
                     q, h = divmod(g, 2)
                     nc.vector.scalar_tensor_tensor(
-                        out=prod[:, q, t, h, :].rearrange("p (c a) -> p c a", a=2),
+                        out=prod[:, q, 2 * (u % 2) + t, h, :].rearrange("p (c a) -> p c a", a=2),
                         in0=qk_tiles[u][:, t, 64 * g : 64 * g + 64].unsqueeze(2).to_broadcast([P, 64, 2]),
                         scalar=rstd_tiles[u][:, 4 * t + g : 4 * t + g + 1],
                         in1=fg_tiles[grp][:, t0 + t, q, :].rearrange("p (c a) -> p c a", a=2),
@@ -307,24 +315,36 @@ def tile_fluxattention_pa_t_kernel(
                         op1=ALU.mult,
                     )
 
-        def stage_add(u):
-            if not valid(u):
-                return
-            if u % 2 == 0:
-                o_new = opool.tile([P, 2, CHUNK_TILES, 128], F32, name="o")
-                o_tiles[u // 2] = o_new
-            o = o_tiles[u // 2]
-            pv = prod_tiles[u][:].rearrange("p q t h (b c) -> p q (t h) b c", b=2)
-            eng = nc.gpsimd if u in GPSIMD_ADDS else nc.vector
+        def add_halves(eng, c, lo, hi):
+            pv = prod_tiles[c][:, :, lo:hi].rearrange("p q t h (b c) -> p q (t h) b c", b=2)
             eng.tensor_tensor(
-                out=o[:, :, 2 * (u % 2) : 2 * (u % 2) + 2, :].rearrange("p q t (h c) -> p q (t h) c", h=2),
+                out=o_tiles[c][:, :, lo:hi, :].rearrange("p q t (h c) -> p q (t h) c", h=2),
                 in0=pv[:, :, :, 0, :],
                 in1=pv[:, :, :, 1, :],
                 op=ALU.add,
             )
+
+        def store_qk(c):
+            nc.sync.dma_start(out=chunk_rows(outs[0], c, 0, CHUNK_TILES), in_=o_tiles[c][:, 0])
+            nc.sync.dma_start(out=chunk_rows(outs[1], c, 0, CHUNK_TILES), in_=o_tiles[c][:, 1])
+
+        def stage_add_vector(c):
+            if not 0 <= c < N_CHUNKS or c not in VECTOR_ADD_CHUNKS:
+                return
+            o_new = opool.tile([P, 2, CHUNK_TILES, 128], F32, name="o")
+            o_tiles[c] = o_new
+            add_halves(nc.vector, c, 0, CHUNK_TILES)
+            store_qk(c)
+
+        def stage_add_gpsimd(u):
+            if not valid(u) or u // 2 in VECTOR_ADD_CHUNKS:
+                return
+            if u % 2 == 0:
+                o_new = opool.tile([P, 2, CHUNK_TILES, 128], F32, name="o")
+                o_tiles[u // 2] = o_new
+            add_halves(nc.gpsimd, u // 2, 2 * (u % 2), 2 * (u % 2) + 2)
             if u % 2 == 1:
-                nc.sync.dma_start(out=chunk_rows(outs[0], u // 2, 0, CHUNK_TILES), in_=o[:, 0])
-                nc.sync.dma_start(out=chunk_rows(outs[1], u // 2, 0, CHUNK_TILES), in_=o[:, 1])
+                store_qk(u // 2)
 
         g_x = [
             [expand_gain(g_raw[0][0], "eq"), expand_gain(g_raw[0][1], "ek")],
@@ -333,24 +353,24 @@ def tile_fluxattention_pa_t_kernel(
         w_q = {}
         w_q[0] = quantise_w(regroup_w(w_raw[0], "we", nc.vector.tensor_copy), "we")
         w_grouped = {}
-        for k in range(GAINS_AT_START):
-            gain_rotary(k)
-        for i in range(-5, N_UNITS + 2):
+        for m in range(GAINS_AT_START):
+            gain_rotary(m)
+        for i in range(-6, N_UNITS + 3):
             stage_rstd(i)
-            stage_copy(i + 4)
-            stage_transpose(i + 5)
+            stage_copy(i + 5)
+            stage_transpose(i + 6)
             stage_square(i + 2)
             stage_v(i + 2)
             stage_products(i - 1)
             stage_reduce(i + 1)
-            stage_quantise(i + 3)
+            if i % 2 == 1:
+                stage_quantise((i + 3) // 2)
+                stage_add_vector((i - 3) // 2)
             stage_matmul(i + 3)
-            stage_add(i - 1)
+            stage_add_gpsimd(i - 1)
             if i == 1:
                 w_grouped[1] = regroup_w(w_raw[1], "wi", nc.scalar.copy)
             if i == 3:
                 w_q[1] = quantise_w(w_grouped[1], "wi")
-            if (i + 7) % 4 == 0 and GAINS_AT_START <= (i + 7) // 2 < 2 * N_GROUPS:
-                gain_rotary((i + 7) // 2)
-            if (i + 5) % 4 == 0 and GAINS_AT_START <= (i + 5) // 2 + 1 < 2 * N_GROUPS:
-                gain_rotary((i + 5) // 2 + 1)
+            if GAINS_AT_START <= i + 6 < 2 * N_CHUNKS:
+                gain_rotary(i + 6)

@@ -22,7 +22,8 @@ UNIT_TILES = 2
 N_UNITS = 32
 CHUNK_TILES = 4
 N_CHUNKS = 16
-VECTOR_ADD_CHUNKS = (0, 2, 4, 6, 8, 10, 12, 14, 15)
+VECTOR_ADD_CHUNKS = (0, 2, 5, 8, 11, 14, 15)
+ACCUM_UNITS = (6, 10, 14, 18, 22, 26, 30)
 GAINS_AT_START = 8
 
 
@@ -127,6 +128,7 @@ def tile_fluxattention_pa_t_kernel(
         warm = const.tile([P, 1], F32, name="warm")
         nc.vector.memset(warm[:], 1.0)
         nc.scalar.activation(out=warm[:], in_=warm[:], func=ACT.Abs_reciprocal_sqrt)
+        junk = const.tile([P, 64], F32, name="junk")
 
         def regroup_w(raw, name, copy):
             grouped = const.tile([P, 384, 4], BF16, name=name + "_grouped", align_bytes=64)
@@ -259,6 +261,17 @@ def tile_fluxattention_pa_t_kernel(
         def stage_square(u):
             if not valid(u):
                 return
+            if u in ACCUM_UNITS:
+                ssq = stat.tile([P, 8], F32, name="ssq")
+                ssq_tiles[u] = ssq
+                for j in range(8):
+                    nc.scalar.activation(
+                        out=junk[:],
+                        in_=qk_tiles[u][:, j // 4, 64 * (j % 4) : 64 * (j % 4) + 64],
+                        func=ACT.Square,
+                        accum_out=ssq[:, j : j + 1],
+                    )
+                return
             sq = sqpool.tile([P, 512], F32, name="sq")
             sq_tiles[u] = sq
             nc.scalar.activation(out=sq[:], in_=qk_tiles[u][:].rearrange("p a c -> p (a c)"), func=ACT.Square)
@@ -275,7 +288,7 @@ def tile_fluxattention_pa_t_kernel(
                 nc.sync.dma_start(out=chunk_rows(outs[2], u // 2, 0, CHUNK_TILES), in_=vsb[:])
 
         def stage_reduce(u):
-            if not valid(u):
+            if not valid(u) or u in ACCUM_UNITS:
                 return
             ssq = stat.tile([P, 8], F32, name="ssq")
             ssq_tiles[u] = ssq

@@ -22,8 +22,7 @@ UNIT_TILES = 2
 N_UNITS = 32
 CHUNK_TILES = 4
 N_CHUNKS = 16
-VECTOR_ADD_CHUNKS = (0, 2, 5, 8, 11, 14, 15)
-ACCUM_UNITS = (6, 10, 14, 18, 22, 26, 30)
+VECTOR_ADD_CHUNKS = (0, 2, 4, 6, 8, 10, 12, 14, 15)
 GAINS_AT_START = 8
 
 
@@ -59,7 +58,7 @@ def tile_fluxattention_pa_t_kernel(
         cpool = ctx.enter_context(tc.tile_pool(name="cpool", bufs=3))
         ppool = ctx.enter_context(tc.tile_pool(name="ppool", bufs=3))
         opool = ctx.enter_context(tc.tile_pool(name="opool", bufs=4))
-        stat = ctx.enter_context(tc.tile_pool(name="stat", bufs=4))
+        stat = ctx.enter_context(tc.tile_pool(name="stat", bufs=8))
         tpsum = ctx.enter_context(tc.psum_pool(name="tpsum", bufs=2))
         qkpsum = ctx.enter_context(tc.psum_pool(name="qkpsum", bufs=4))
         vpsum = ctx.enter_context(tc.psum_pool(name="vpsum", bufs=2))
@@ -128,15 +127,17 @@ def tile_fluxattention_pa_t_kernel(
         warm = const.tile([P, 1], F32, name="warm")
         nc.vector.memset(warm[:], 1.0)
         nc.scalar.activation(out=warm[:], in_=warm[:], func=ACT.Abs_reciprocal_sqrt)
-        junk = const.tile([P, 64], F32, name="junk")
 
         def regroup_w(raw, name, copy):
             grouped = const.tile([P, 384, 4], BF16, name=name + "_grouped", align_bytes=64)
-            for b in range(2):
-                copy(
-                    out=grouped[:, 0:256, :].rearrange("p (g b i) t -> p g b i t", g=4, b=2, i=32)[:, :, b],
-                    in_=raw[:, :, 0:256].rearrange("p t (g i b) -> p g b i t", g=4, i=32, b=2)[:, :, b],
-                )
+            for h in range(2):
+                for b in range(2):
+                    copy(
+                        out=grouped[:, 0:256, :].rearrange("p (h q b i) t -> p h b q i t", h=2, q=2, b=2, i=32)[
+                            :, h, b
+                        ],
+                        in_=raw[:, :, 0:256].rearrange("p t (q h i b) -> p h b q i t", q=2, h=2, i=32, b=2)[:, h, b],
+                    )
             copy(out=grouped[:, 256:384, :], in_=raw[:, :, 256:384].rearrange("p t n -> p n t"))
             return grouped
 
@@ -261,17 +262,6 @@ def tile_fluxattention_pa_t_kernel(
         def stage_square(u):
             if not valid(u):
                 return
-            if u in ACCUM_UNITS:
-                ssq = stat.tile([P, 8], F32, name="ssq")
-                ssq_tiles[u] = ssq
-                for j in range(8):
-                    nc.scalar.activation(
-                        out=junk[:],
-                        in_=qk_tiles[u][:, j // 4, 64 * (j % 4) : 64 * (j % 4) + 64],
-                        func=ACT.Square,
-                        accum_out=ssq[:, j : j + 1],
-                    )
-                return
             sq = sqpool.tile([P, 512], F32, name="sq")
             sq_tiles[u] = sq
             nc.scalar.activation(out=sq[:], in_=qk_tiles[u][:].rearrange("p a c -> p (a c)"), func=ACT.Square)
@@ -288,7 +278,7 @@ def tile_fluxattention_pa_t_kernel(
                 nc.sync.dma_start(out=chunk_rows(outs[2], u // 2, 0, CHUNK_TILES), in_=vsb[:])
 
         def stage_reduce(u):
-            if not valid(u) or u in ACCUM_UNITS:
+            if not valid(u):
                 return
             ssq = stat.tile([P, 8], F32, name="ssq")
             ssq_tiles[u] = ssq
@@ -313,25 +303,27 @@ def tile_fluxattention_pa_t_kernel(
                 return
             grp, t0 = divmod(2 * u, GROUP_TILES)
             if u % 2 == 0:
-                prod_new = ppool.tile([P, 2, CHUNK_TILES, 2, 128], F32, name="prod")
+                prod_new = ppool.tile([P, CHUNK_TILES, 2, 2, 128], F32, name="prod")
                 prod_tiles[u // 2] = prod_new
             prod = prod_tiles[u // 2]
             for t in range(2):
-                for g in range(4):
-                    q, h = divmod(g, 2)
-                    nc.vector.scalar_tensor_tensor(
-                        out=prod[:, q, 2 * (u % 2) + t, h, :].rearrange("p (c a) -> p c a", a=2),
-                        in0=qk_tiles[u][:, t, 64 * g : 64 * g + 64].unsqueeze(2).to_broadcast([P, 64, 2]),
-                        scalar=rstd_tiles[u][:, 4 * t + g : 4 * t + g + 1],
-                        in1=fg_tiles[grp][:, t0 + t, q, :].rearrange("p (c a) -> p c a", a=2),
-                        op0=ALU.mult,
-                        op1=ALU.mult,
-                    )
+                nc.vector.tensor_tensor(
+                    out=prod[:, 2 * (u % 2) + t].rearrange("p h q (c a) -> p h (q c) a", a=2),
+                    in0=qk_tiles[u][:, t, :]
+                    .rearrange("p (h x) -> p h x", h=2)
+                    .unsqueeze(3)
+                    .to_broadcast([P, 2, 128, 2]),
+                    in1=fg_tiles[grp][:, t0 + t]
+                    .rearrange("p q (c a) -> p (q c) a", a=2)
+                    .unsqueeze(1)
+                    .to_broadcast([P, 2, 128, 2]),
+                    op=ALU.mult,
+                )
 
         def add_halves(eng, c, lo, hi):
-            pv = prod_tiles[c][:, :, lo:hi].rearrange("p q t h (b c) -> p q (t h) b c", b=2)
+            pv = prod_tiles[c][:, lo:hi].rearrange("p t h q (b c) -> p (t h) q b c", b=2)
             eng.tensor_tensor(
-                out=o_tiles[c][:, :, lo:hi, :].rearrange("p q t (h c) -> p q (t h) c", h=2),
+                out=o_tiles[c][:, :, lo:hi, :].rearrange("p q t (h c) -> p (t h) q c", h=2),
                 in0=pv[:, :, :, 0, :],
                 in1=pv[:, :, :, 1, :],
                 op=ALU.add,
@@ -347,7 +339,6 @@ def tile_fluxattention_pa_t_kernel(
             o_new = opool.tile([P, 2, CHUNK_TILES, 128], F32, name="o")
             o_tiles[c] = o_new
             add_halves(nc.vector, c, 0, CHUNK_TILES)
-            store_qk(c)
 
         def stage_add_gpsimd(u):
             if not valid(u) or u // 2 in VECTOR_ADD_CHUNKS:
@@ -356,6 +347,17 @@ def tile_fluxattention_pa_t_kernel(
                 o_new = opool.tile([P, 2, CHUNK_TILES, 128], F32, name="o")
                 o_tiles[u // 2] = o_new
             add_halves(nc.gpsimd, u // 2, 2 * (u % 2), 2 * (u % 2) + 2)
+
+        def stage_scale(u):
+            if not valid(u):
+                return
+            o = o_tiles[u // 2]
+            for t in range(2):
+                for h in range(2):
+                    for q in range(2):
+                        rows = o[:, q, 2 * (u % 2) + t, 64 * h : 64 * h + 64]
+                        j = 4 * t + 2 * h + q
+                        nc.scalar.activation(out=rows, in_=rows, func=ACT.Copy, scale=rstd_tiles[u][:, j : j + 1])
             if u % 2 == 1:
                 store_qk(u // 2)
 
@@ -368,19 +370,20 @@ def tile_fluxattention_pa_t_kernel(
         w_grouped = {}
         for m in range(GAINS_AT_START):
             gain_rotary(m)
-        for i in range(-6, N_UNITS + 3):
+        for i in range(-6, N_UNITS + 5):
             stage_rstd(i)
             stage_copy(i + 5)
             stage_transpose(i + 6)
             stage_square(i + 2)
             stage_v(i + 2)
-            stage_products(i - 1)
+            stage_scale(i - 4)
+            stage_products(i + 1)
             stage_reduce(i + 1)
             if i % 2 == 1:
                 stage_quantise((i + 3) // 2)
-                stage_add_vector((i - 3) // 2)
+                stage_add_vector((i - 1) // 2)
             stage_matmul(i + 3)
-            stage_add_gpsimd(i - 1)
+            stage_add_gpsimd(i)
             if i == 1:
                 w_grouped[1] = regroup_w(w_raw[1], "wi", nc.scalar.copy)
             if i == 3:

@@ -22,7 +22,9 @@ UNIT_TILES = 2
 N_UNITS = 32
 CHUNK_TILES = 4
 N_CHUNKS = 16
-VECTOR_ADD_CHUNKS = (0, 2, 4, 6, 8, 10, 12, 14, 15)
+VECTOR_ADD_CHUNKS = (0, 1, 3, 4, 6, 7, 9, 10, 12, 14)
+LAST_CHUNK = 15
+ACCUM_UNITS = (2, 5, 8, 11, 14, 17, 20, 23, 26, 29)
 GAINS_AT_START = 8
 
 
@@ -58,7 +60,7 @@ def tile_fluxattention_pa_t_kernel(
         cpool = ctx.enter_context(tc.tile_pool(name="cpool", bufs=3))
         ppool = ctx.enter_context(tc.tile_pool(name="ppool", bufs=3))
         opool = ctx.enter_context(tc.tile_pool(name="opool", bufs=4))
-        stat = ctx.enter_context(tc.tile_pool(name="stat", bufs=8))
+        stat = ctx.enter_context(tc.tile_pool(name="stat", bufs=4))
         tpsum = ctx.enter_context(tc.psum_pool(name="tpsum", bufs=2))
         qkpsum = ctx.enter_context(tc.psum_pool(name="qkpsum", bufs=4))
         vpsum = ctx.enter_context(tc.psum_pool(name="vpsum", bufs=2))
@@ -96,12 +98,15 @@ def tile_fluxattention_pa_t_kernel(
                 )
             return xt
 
+        def load_f_part(ft, grp, lo, hi):
+            nc.sync.dma_start(
+                out=ft[:, lo:hi, :],
+                in_=rot[1024 * grp : 1024 * grp + 1024, :].rearrange("(p t) f -> p t f", t=GROUP_TILES)[:, lo:hi, :],
+            )
+
         def load_f(grp):
             ft = fpool.tile([P, GROUP_TILES, 128], BF16, name="f")
-            nc.sync.dma_start(
-                out=ft[:],
-                in_=rot[1024 * grp : 1024 * grp + 1024, :].rearrange("(p t) f -> p t f", t=GROUP_TILES),
-            )
+            load_f_part(ft, grp, 0, GROUP_TILES)
             return ft
 
         g_raw = [
@@ -111,9 +116,12 @@ def tile_fluxattention_pa_t_kernel(
         x_tiles = {}
         f_tiles = {}
         w_raw = {}
+        f_first = fpool.tile([P, GROUP_TILES, 128], BF16, name="f")
+        f_tiles[0] = f_first
+        load_f_part(f_first, 0, 0, CHUNK_TILES)
         w_raw[0] = load_w(W_eqkv, "we")
         x_tiles[0] = load_x(0, 2)
-        f_tiles[0] = load_f(0)
+        load_f_part(f_first, 0, CHUNK_TILES, GROUP_TILES)
         x_tiles[1] = load_x(1, 1)
         w_raw[1] = load_w(W_iqkv, "wi")
         f_tiles[1] = load_f(1)
@@ -127,17 +135,15 @@ def tile_fluxattention_pa_t_kernel(
         warm = const.tile([P, 1], F32, name="warm")
         nc.vector.memset(warm[:], 1.0)
         nc.scalar.activation(out=warm[:], in_=warm[:], func=ACT.Abs_reciprocal_sqrt)
+        junk = const.tile([P, 64], F32, name="junk")
 
         def regroup_w(raw, name, copy):
             grouped = const.tile([P, 384, 4], BF16, name=name + "_grouped", align_bytes=64)
-            for h in range(2):
-                for b in range(2):
-                    copy(
-                        out=grouped[:, 0:256, :].rearrange("p (h q b i) t -> p h b q i t", h=2, q=2, b=2, i=32)[
-                            :, h, b
-                        ],
-                        in_=raw[:, :, 0:256].rearrange("p t (q h i b) -> p h b q i t", q=2, h=2, i=32, b=2)[:, h, b],
-                    )
+            for b in range(2):
+                copy(
+                    out=grouped[:, 0:256, :].rearrange("p (g b i) t -> p g b i t", g=4, b=2, i=32)[:, :, b],
+                    in_=raw[:, :, 0:256].rearrange("p t (g i b) -> p g b i t", g=4, i=32, b=2)[:, :, b],
+                )
             copy(out=grouped[:, 256:384, :], in_=raw[:, :, 256:384].rearrange("p t n -> p n t"))
             return grouped
 
@@ -262,6 +268,17 @@ def tile_fluxattention_pa_t_kernel(
         def stage_square(u):
             if not valid(u):
                 return
+            if u in ACCUM_UNITS:
+                ssq = stat.tile([P, 8], F32, name="ssq")
+                ssq_tiles[u] = ssq
+                for j in range(8):
+                    nc.scalar.activation(
+                        out=junk[:],
+                        in_=qk_tiles[u][:, j // 4, 64 * (j % 4) : 64 * (j % 4) + 64],
+                        func=ACT.Square,
+                        accum_out=ssq[:, j : j + 1],
+                    )
+                return
             sq = sqpool.tile([P, 512], F32, name="sq")
             sq_tiles[u] = sq
             nc.scalar.activation(out=sq[:], in_=qk_tiles[u][:].rearrange("p a c -> p (a c)"), func=ACT.Square)
@@ -278,7 +295,7 @@ def tile_fluxattention_pa_t_kernel(
                 nc.sync.dma_start(out=chunk_rows(outs[2], u // 2, 0, CHUNK_TILES), in_=vsb[:])
 
         def stage_reduce(u):
-            if not valid(u):
+            if not valid(u) or u in ACCUM_UNITS:
                 return
             ssq = stat.tile([P, 8], F32, name="ssq")
             ssq_tiles[u] = ssq
@@ -303,27 +320,25 @@ def tile_fluxattention_pa_t_kernel(
                 return
             grp, t0 = divmod(2 * u, GROUP_TILES)
             if u % 2 == 0:
-                prod_new = ppool.tile([P, CHUNK_TILES, 2, 2, 128], F32, name="prod")
+                prod_new = ppool.tile([P, 2, CHUNK_TILES, 2, 128], F32, name="prod")
                 prod_tiles[u // 2] = prod_new
             prod = prod_tiles[u // 2]
             for t in range(2):
-                nc.vector.tensor_tensor(
-                    out=prod[:, 2 * (u % 2) + t].rearrange("p h q (c a) -> p h (q c) a", a=2),
-                    in0=qk_tiles[u][:, t, :]
-                    .rearrange("p (h x) -> p h x", h=2)
-                    .unsqueeze(3)
-                    .to_broadcast([P, 2, 128, 2]),
-                    in1=fg_tiles[grp][:, t0 + t]
-                    .rearrange("p q (c a) -> p (q c) a", a=2)
-                    .unsqueeze(1)
-                    .to_broadcast([P, 2, 128, 2]),
-                    op=ALU.mult,
-                )
+                for g in range(4):
+                    q, h = divmod(g, 2)
+                    nc.vector.scalar_tensor_tensor(
+                        out=prod[:, q, 2 * (u % 2) + t, h, :].rearrange("p (c a) -> p c a", a=2),
+                        in0=qk_tiles[u][:, t, 64 * g : 64 * g + 64].unsqueeze(2).to_broadcast([P, 64, 2]),
+                        scalar=rstd_tiles[u][:, 4 * t + g : 4 * t + g + 1],
+                        in1=fg_tiles[grp][:, t0 + t, q, :].rearrange("p (c a) -> p c a", a=2),
+                        op0=ALU.mult,
+                        op1=ALU.mult,
+                    )
 
         def add_halves(eng, c, lo, hi):
-            pv = prod_tiles[c][:, lo:hi].rearrange("p t h q (b c) -> p (t h) q b c", b=2)
+            pv = prod_tiles[c][:, :, lo:hi].rearrange("p q t h (b c) -> p q (t h) b c", b=2)
             eng.tensor_tensor(
-                out=o_tiles[c][:, :, lo:hi, :].rearrange("p q t (h c) -> p (t h) q c", h=2),
+                out=o_tiles[c][:, :, lo:hi, :].rearrange("p q t (h c) -> p q (t h) c", h=2),
                 in0=pv[:, :, :, 0, :],
                 in1=pv[:, :, :, 1, :],
                 op=ALU.add,
@@ -339,25 +354,26 @@ def tile_fluxattention_pa_t_kernel(
             o_new = opool.tile([P, 2, CHUNK_TILES, 128], F32, name="o")
             o_tiles[c] = o_new
             add_halves(nc.vector, c, 0, CHUNK_TILES)
+            store_qk(c)
+
+        def stage_add_last(u):
+            if not valid(u) or u // 2 != LAST_CHUNK:
+                return
+            if u % 2 == 0:
+                o_new = opool.tile([P, 2, CHUNK_TILES, 128], F32, name="o")
+                o_tiles[LAST_CHUNK] = o_new
+            lo = 2 * (u % 2)
+            add_halves(nc.vector, LAST_CHUNK, lo, lo + 2)
+            nc.sync.dma_start(out=chunk_rows(outs[0], LAST_CHUNK, lo, lo + 2), in_=o_tiles[LAST_CHUNK][:, 0, lo : lo + 2, :])
+            nc.sync.dma_start(out=chunk_rows(outs[1], LAST_CHUNK, lo, lo + 2), in_=o_tiles[LAST_CHUNK][:, 1, lo : lo + 2, :])
 
         def stage_add_gpsimd(u):
-            if not valid(u) or u // 2 in VECTOR_ADD_CHUNKS:
+            if not valid(u) or u // 2 in VECTOR_ADD_CHUNKS or u // 2 == LAST_CHUNK:
                 return
             if u % 2 == 0:
                 o_new = opool.tile([P, 2, CHUNK_TILES, 128], F32, name="o")
                 o_tiles[u // 2] = o_new
             add_halves(nc.gpsimd, u // 2, 2 * (u % 2), 2 * (u % 2) + 2)
-
-        def stage_scale(u):
-            if not valid(u):
-                return
-            o = o_tiles[u // 2]
-            for t in range(2):
-                for h in range(2):
-                    for q in range(2):
-                        rows = o[:, q, 2 * (u % 2) + t, 64 * h : 64 * h + 64]
-                        j = 4 * t + 2 * h + q
-                        nc.scalar.activation(out=rows, in_=rows, func=ACT.Copy, scale=rstd_tiles[u][:, j : j + 1])
             if u % 2 == 1:
                 store_qk(u // 2)
 
@@ -370,20 +386,20 @@ def tile_fluxattention_pa_t_kernel(
         w_grouped = {}
         for m in range(GAINS_AT_START):
             gain_rotary(m)
-        for i in range(-6, N_UNITS + 5):
+        for i in range(-6, N_UNITS + 3):
             stage_rstd(i)
             stage_copy(i + 5)
             stage_transpose(i + 6)
             stage_square(i + 2)
             stage_v(i + 2)
-            stage_scale(i - 4)
-            stage_products(i + 1)
+            stage_products(i - 1)
+            stage_add_last(i - 1)
             stage_reduce(i + 1)
             if i % 2 == 1:
                 stage_quantise((i + 3) // 2)
-                stage_add_vector((i - 1) // 2)
+                stage_add_vector((i - 3) // 2)
             stage_matmul(i + 3)
-            stage_add_gpsimd(i)
+            stage_add_gpsimd(i - 1)
             if i == 1:
                 w_grouped[1] = regroup_w(w_raw[1], "wi", nc.scalar.copy)
             if i == 3:

from contextlib import ExitStack

import concourse.mybir as mybir
from concourse.masks import make_identity

FLOPS = 2 * 8192 * 512 * 384

F32 = mybir.dt.float32
BF16 = mybir.dt.bfloat16
U32 = mybir.dt.uint32
U8 = mybir.dt.uint8
FP8X4 = mybir.dt.float8_e4m3fn_x4
ALU = mybir.AluOpType
ACT = mybir.ActivationFunctionType

P = 128
EPS = 1e-6
GROUP_TILES = 8
N_GROUPS = 8
TEXT_GROUPS = 2
UNIT_TILES = 2
N_UNITS = 32
CHUNK_TILES = 4
N_CHUNKS = 16
VECTOR_ADD_CHUNKS = (0, 1, 3, 4, 6, 7, 9, 10, 12, 14)
LAST_CHUNK = 15
ACCUM_UNITS = (2, 5, 8, 11, 14, 17, 20, 23, 26, 29)
GAINS_AT_START = 8


def tile_fluxattention_pa_t_kernel(
    tc,
    hidden_states,
    encoder_hidden_states,
    image_rotary_emb,
    W_iqkv,
    W_eqkv,
    qn_scale,
    kn_scale,
    eqn_scale,
    ekn_scale,
    out_0,
    out_1,
    out_2,
):
    nc = tc.nc
    x_img = hidden_states.flatten_outer_dims()
    x_txt = encoder_hidden_states.flatten_outer_dims()
    rot = image_rotary_emb.rearrange("l i f -> l (i f)")
    outs = [out_0.flatten_outer_dims(), out_1.flatten_outer_dims(), out_2.flatten_outer_dims()]

    with ExitStack() as ctx:
        ctx.enter_context(tc.manual_schedule())
        const = ctx.enter_context(tc.tile_pool(name="const", bufs=1))
        xpool = ctx.enter_context(tc.tile_pool(name="xpool", bufs=N_CHUNKS))
        fpool = ctx.enter_context(tc.tile_pool(name="fpool", bufs=N_GROUPS))
        fgpool = ctx.enter_context(tc.tile_pool(name="fgpool", bufs=4))
        sqpool = ctx.enter_context(tc.tile_pool(name="sqpool", bufs=3))
        gpool = ctx.enter_context(tc.tile_pool(name="gpool", bufs=3))
        cpool = ctx.enter_context(tc.tile_pool(name="cpool", bufs=3))
        ppool = ctx.enter_context(tc.tile_pool(name="ppool", bufs=3))
        opool = ctx.enter_context(tc.tile_pool(name="opool", bufs=4))
        stat = ctx.enter_context(tc.tile_pool(name="stat", bufs=4))
        tpsum = ctx.enter_context(tc.psum_pool(name="tpsum", bufs=2))
        qkpsum = ctx.enter_context(tc.psum_pool(name="qkpsum", bufs=4))
        vpsum = ctx.enter_context(tc.psum_pool(name="vpsum", bufs=2))

        def chunk_rows(dram, c, lo, hi):
            grp, half = divmod(c, 2)
            return dram[1024 * grp : 1024 * grp + 1024, :].rearrange("(p t) f -> p t f", t=GROUP_TILES)[
                :, 4 * half + lo : 4 * half + hi, :
            ]

        def load_gain(g, name):
            raw = const.tile([P, 64], BF16, name=name + "_raw")
            nc.scalar.dma_start(out=raw[:], in_=g.partition_broadcast(P))
            return raw

        def load_w(w, name):
            raw = const.tile([P, 4, 384], BF16, name=name + "_raw")
            for half in range(2):
                nc.sync.dma_start(
                    out=raw[:, 2 * half : 2 * half + 2, :],
                    in_=w[256 * half : 256 * half + 256, :].rearrange("(p e) c -> p e c", e=2),
                )
            return raw

        def load_x(c, pieces):
            if c < 2 * TEXT_GROUPS:
                src, cc = x_txt, c
            else:
                src, cc = x_img, c - 2 * TEXT_GROUPS
            xt = xpool.tile([P, CHUNK_TILES, 512], BF16, name="x")
            step = CHUNK_TILES // pieces
            for k in range(pieces):
                nc.sync.dma_start(
                    out=xt[:, step * k : step * k + step, :], in_=chunk_rows(src, cc, step * k, step * k + step)
                )
            return xt

        def load_f_part(ft, grp, lo, hi):
            nc.sync.dma_start(
                out=ft[:, lo:hi, :],
                in_=rot[1024 * grp : 1024 * grp + 1024, :].rearrange("(p t) f -> p t f", t=GROUP_TILES)[:, lo:hi, :],
            )

        def load_f(grp):
            ft = fpool.tile([P, GROUP_TILES, 128], BF16, name="f")
            load_f_part(ft, grp, 0, GROUP_TILES)
            return ft

        g_raw = [
            [load_gain(eqn_scale, "eq"), load_gain(ekn_scale, "ek")],
            [load_gain(qn_scale, "iq"), load_gain(kn_scale, "ik")],
        ]
        x_tiles = {}
        f_tiles = {}
        w_raw = {}
        f_first = fpool.tile([P, GROUP_TILES, 128], BF16, name="f")
        f_tiles[0] = f_first
        load_f_part(f_first, 0, 0, CHUNK_TILES)
        w_raw[0] = load_w(W_eqkv, "we")
        x_tiles[0] = load_x(0, 2)
        load_f_part(f_first, 0, CHUNK_TILES, GROUP_TILES)
        x_tiles[1] = load_x(1, 1)
        w_raw[1] = load_w(W_iqkv, "wi")
        f_tiles[1] = load_f(1)
        for c in range(2, N_CHUNKS):
            x_tiles[c] = load_x(c, 1)
            if c < N_GROUPS:
                f_tiles[c] = load_f(c)

        ident = const.tile([P, P], F32, name="ident")
        make_identity(nc, ident[:])
        warm = const.tile([P, 1], F32, name="warm")
        nc.vector.memset(warm[:], 1.0)
        nc.scalar.activation(out=warm[:], in_=warm[:], func=ACT.Abs_reciprocal_sqrt)
        junk = const.tile([P, 64], F32, name="junk")

        def regroup_w(raw, name, copy):
            grouped = const.tile([P, 384, 4], BF16, name=name + "_grouped", align_bytes=64)
            for b in range(2):
                copy(
                    out=grouped[:, 0:256, :].rearrange("p (g b i) t -> p g b i t", g=4, b=2, i=32)[:, :, b],
                    in_=raw[:, :, 0:256].rearrange("p t (g i b) -> p g b i t", g=4, i=32, b=2)[:, :, b],
                )
            copy(out=grouped[:, 256:384, :], in_=raw[:, :, 256:384].rearrange("p t n -> p n t"))
            return grouped

        def quantise_w(grouped, name):
            codes = const.tile([P, 384], U32, name=name + "_codes", align_bytes=64)
            scales = const.tile([P, 384], U8, name=name + "_scales", align_bytes=64)
            for lo, hi in ((0, 256), (256, 384)):
                nc.vector.quantize_mx(
                    out=codes[:, lo:hi].bitcast(FP8X4),
                    scales=scales[:, lo:hi],
                    in_=grouped[:, lo:hi, :].rearrange("p n t -> p (n t)"),
                )
            return codes, scales

        def expand_gain(raw, name):
            gx = const.tile([P, 2, 32, 2], BF16, name=name + "_gx")
            nc.vector.tensor_copy(
                out=gx[:],
                in_=raw[:].rearrange("p (i b) -> p b i", b=2).unsqueeze(3).to_broadcast([P, 2, 32, 2]),
            )
            return gx

        fg_tiles = {}

        def gain_rotary(m):
            c, q = divmod(m, 2)
            grp, half = divmod(c, 2)
            s = 0 if grp < TEXT_GROUPS else 1
            if m % 4 == 0:
                fg_new = fgpool.tile([P, GROUP_TILES, 2, 128], F32, name="fg")
                fg_tiles[grp] = fg_new
            tiles = slice(4 * half, 4 * half + 4)
            nc.gpsimd.tensor_tensor(
                out=fg_tiles[grp][:, tiles, q, :].rearrange("p n (b c) -> p n b c", b=2),
                in0=f_tiles[grp][:, tiles, :].rearrange("p n (c b) -> p n b c", b=2),
                in1=g_x[s][q][:]
                .rearrange("p b i a -> p b (i a)")
                .unsqueeze(1)
                .to_broadcast([P, CHUNK_TILES, 2, 64]),
                op=ALU.mult,
            )

        xt_tiles = {}
        xg_tiles = {}
        xq_tiles = {}
        qk_tiles = {}
        v_tiles = {}
        sq_tiles = {}
        ssq_tiles = {}
        rstd_tiles = {}
        prod_tiles = {}
        o_tiles = {}
        vsb_tiles = {}

        def valid(u):
            return 0 <= u < N_UNITS

        def stage_transpose(u):
            if not valid(u):
                return
            xw = x_tiles[u // 2][:].bitcast(F32)
            xt = tpsum.tile([P, 2, 2, 128], F32, name="xt")
            xt_tiles[u] = xt
            for a in range(2):
                for half in range(2):
                    nc.tensor.transpose(
                        xt[:, a, half, :], xw[:, 2 * (u % 2) + a, 128 * half : 128 * half + 128], ident[:]
                    )

        def stage_copy(u):
            if not valid(u):
                return
            if u % 2 == 0:
                xg_new = gpool.tile([P, 2048], BF16, name="xg", align_bytes=64)
                xg_tiles[u // 2] = xg_new
            xg = xg_tiles[u // 2]
            nc.scalar.copy(
                out=xg[:, 1024 * (u % 2) : 1024 * (u % 2) + 1024]
                .bitcast(F32)
                .rearrange("p (a r h) -> p a r h", a=2, r=128, h=2),
                in_=xt_tiles[u][:].rearrange("p a h r -> p a r h"),
            )

        def stage_quantise(c):
            if not 0 <= c < N_CHUNKS:
                return
            xc = cpool.tile([P, 512], U32, name="xc", align_bytes=64)
            xs = cpool.tile([P, 512], U8, name="xs", align_bytes=64)
            nc.vector.quantize_mx(out=xc[:].bitcast(FP8X4), scales=xs[:], in_=xg_tiles[c][:])
            xq_tiles[c] = (xc, xs)

        def stage_matmul(u):
            if not valid(u):
                return
            wc, ws = w_q[0 if u < 4 * TEXT_GROUPS else 1]
            xc, xs = xq_tiles[u // 2]
            vps = vpsum.tile([P, 2, 128], F32, name="vps")
            v_tiles[u] = vps
            qk = qkpsum.tile([P, 2, 256], F32, name="qk")
            qk_tiles[u] = qk
            for a in range(2):
                cols = slice(256 * (u % 2) + 128 * a, 256 * (u % 2) + 128 * a + 128)
                nc.tensor.matmul_mx(
                    out=qk[:, a, :],
                    lhsT=xc[:, cols].bitcast(FP8X4),
                    lhsT_scale=xs[:, cols],
                    rhs=wc[:, 0:256].bitcast(FP8X4),
                    rhs_scale=ws[:, 0:256],
                    start=True,
                    stop=True,
                )
                nc.tensor.matmul_mx(
                    out=vps[:, a, :],
                    lhsT=xc[:, cols].bitcast(FP8X4),
                    lhsT_scale=xs[:, cols],
                    rhs=wc[:, 256:384].bitcast(FP8X4),
                    rhs_scale=ws[:, 256:384],
                    start=True,
                    stop=True,
                )

        def stage_square(u):
            if not valid(u):
                return
            if u in ACCUM_UNITS:
                ssq = stat.tile([P, 8], F32, name="ssq")
                ssq_tiles[u] = ssq
                for j in range(8):
                    nc.scalar.activation(
                        out=junk[:],
                        in_=qk_tiles[u][:, j // 4, 64 * (j % 4) : 64 * (j % 4) + 64],
                        func=ACT.Square,
                        accum_out=ssq[:, j : j + 1],
                    )
                return
            sq = sqpool.tile([P, 512], F32, name="sq")
            sq_tiles[u] = sq
            nc.scalar.activation(out=sq[:], in_=qk_tiles[u][:].rearrange("p a c -> p (a c)"), func=ACT.Square)

        def stage_v(u):
            if not valid(u):
                return
            if u % 2 == 0:
                vsb_new = opool.tile([P, CHUNK_TILES, 128], F32, name="vsb")
                vsb_tiles[u // 2] = vsb_new
            vsb = vsb_tiles[u // 2]
            nc.scalar.copy(out=vsb[:, 2 * (u % 2) : 2 * (u % 2) + 2, :], in_=v_tiles[u][:])
            if u % 2 == 1:
                nc.sync.dma_start(out=chunk_rows(outs[2], u // 2, 0, CHUNK_TILES), in_=vsb[:])

        def stage_reduce(u):
            if not valid(u) or u in ACCUM_UNITS:
                return
            ssq = stat.tile([P, 8], F32, name="ssq")
            ssq_tiles[u] = ssq
            nc.vector.tensor_reduce(
                out=ssq[:],
                in_=sq_tiles[u][:].rearrange("p (g c) -> p g c", c=64),
                axis=mybir.AxisListType.X,
                op=ALU.add,
            )

        def stage_rstd(u):
            if not valid(u):
                return
            rstd = stat.tile([P, 8], F32, name="rstd")
            nc.scalar.activation(
                out=rstd[:], in_=ssq_tiles[u][:], func=ACT.Abs_reciprocal_sqrt, scale=1.0 / 64.0, bias=EPS
            )
            rstd_tiles[u] = rstd

        def stage_products(u):
            if not valid(u):
                return
            grp, t0 = divmod(2 * u, GROUP_TILES)
            if u % 2 == 0:
                prod_new = ppool.tile([P, 2, CHUNK_TILES, 2, 128], F32, name="prod")
                prod_tiles[u // 2] = prod_new
            prod = prod_tiles[u // 2]
            for t in range(2):
                for g in range(4):
                    q, h = divmod(g, 2)
                    nc.vector.scalar_tensor_tensor(
                        out=prod[:, q, 2 * (u % 2) + t, h, :].rearrange("p (c a) -> p c a", a=2),
                        in0=qk_tiles[u][:, t, 64 * g : 64 * g + 64].unsqueeze(2).to_broadcast([P, 64, 2]),
                        scalar=rstd_tiles[u][:, 4 * t + g : 4 * t + g + 1],
                        in1=fg_tiles[grp][:, t0 + t, q, :].rearrange("p (c a) -> p c a", a=2),
                        op0=ALU.mult,
                        op1=ALU.mult,
                    )

        def add_halves(eng, c, lo, hi):
            pv = prod_tiles[c][:, :, lo:hi].rearrange("p q t h (b c) -> p q (t h) b c", b=2)
            eng.tensor_tensor(
                out=o_tiles[c][:, :, lo:hi, :].rearrange("p q t (h c) -> p q (t h) c", h=2),
                in0=pv[:, :, :, 0, :],
                in1=pv[:, :, :, 1, :],
                op=ALU.add,
            )

        def store_qk(c):
            nc.sync.dma_start(out=chunk_rows(outs[0], c, 0, CHUNK_TILES), in_=o_tiles[c][:, 0])
            nc.sync.dma_start(out=chunk_rows(outs[1], c, 0, CHUNK_TILES), in_=o_tiles[c][:, 1])

        def stage_add_vector(c):
            if not 0 <= c < N_CHUNKS or c not in VECTOR_ADD_CHUNKS:
                return
            o_new = opool.tile([P, 2, CHUNK_TILES, 128], F32, name="o")
            o_tiles[c] = o_new
            add_halves(nc.vector, c, 0, CHUNK_TILES)
            store_qk(c)

        def stage_add_last(u):
            if not valid(u) or u // 2 != LAST_CHUNK:
                return
            if u % 2 == 0:
                o_new = opool.tile([P, 2, CHUNK_TILES, 128], F32, name="o")
                o_tiles[LAST_CHUNK] = o_new
            lo = 2 * (u % 2)
            add_halves(nc.vector, LAST_CHUNK, lo, lo + 2)
            nc.sync.dma_start(out=chunk_rows(outs[0], LAST_CHUNK, lo, lo + 2), in_=o_tiles[LAST_CHUNK][:, 0, lo : lo + 2, :])
            nc.sync.dma_start(out=chunk_rows(outs[1], LAST_CHUNK, lo, lo + 2), in_=o_tiles[LAST_CHUNK][:, 1, lo : lo + 2, :])

        def stage_add_gpsimd(u):
            if not valid(u) or u // 2 in VECTOR_ADD_CHUNKS or u // 2 == LAST_CHUNK:
                return
            if u % 2 == 0:
                o_new = opool.tile([P, 2, CHUNK_TILES, 128], F32, name="o")
                o_tiles[u // 2] = o_new
            add_halves(nc.gpsimd, u // 2, 2 * (u % 2), 2 * (u % 2) + 2)
            if u % 2 == 1:
                store_qk(u // 2)

        g_x = [
            [expand_gain(g_raw[0][0], "eq"), expand_gain(g_raw[0][1], "ek")],
            [expand_gain(g_raw[1][0], "iq"), expand_gain(g_raw[1][1], "ik")],
        ]
        w_q = {}
        w_q[0] = quantise_w(regroup_w(w_raw[0], "we", nc.vector.tensor_copy), "we")
        w_grouped = {}
        for m in range(GAINS_AT_START):
            gain_rotary(m)
        for i in range(-6, N_UNITS + 3):
            stage_rstd(i)
            stage_copy(i + 5)
            stage_transpose(i + 6)
            stage_square(i + 2)
            stage_v(i + 2)
            stage_products(i - 1)
            stage_add_last(i - 1)
            stage_reduce(i + 1)
            if i % 2 == 1:
                stage_quantise((i + 3) // 2)
                stage_add_vector((i - 3) // 2)
            stage_matmul(i + 3)
            stage_add_gpsimd(i - 1)
            if i == 1:
                w_grouped[1] = regroup_w(w_raw[1], "wi", nc.scalar.copy)
            if i == 3:
                w_q[1] = quantise_w(w_grouped[1], "wi")
            if GAINS_AT_START <= i + 6 < 2 * N_CHUNKS:
                gain_rotary(i + 6)
